import numpy as np
import ml_dtypes


def mxq(x, axis, fmt="e4m3"):
    dtype, down = {"e4m3": (ml_dtypes.float8_e4m3fn, 7), "e5m2": (ml_dtypes.float8_e5m2, 14)}[fmt]
    v = np.moveaxis(np.asarray(x, np.float32).astype(ml_dtypes.bfloat16).astype(np.float64), axis, -1)
    blocks = v.reshape(v.shape[:-1] + (-1, 32))
    amax = np.abs(blocks).max(-1, keepdims=True)
    byte = np.maximum(np.where(amax > 0, np.frexp(amax)[1] - 1 + 127, 0) - down, 1)
    scale = np.exp2(byte - 127.0)
    codes = (blocks / scale).astype(np.float32).astype(dtype).astype(np.float64)
    return np.moveaxis((codes * scale).reshape(v.shape), -1, axis)


WIDE = False


def mx_kscale(k):
    if not WIDE:
        return np.ones(k)
    levels = np.array([10, -10, 5, -5, 0])
    if k % 512:
        return np.exp2(np.random.permutation(np.resize(levels, k // 32))).repeat(32)
    a = np.empty((k // 512, 16))
    for p in range(k // 512):
        a[p, :8] = np.random.permutation(np.resize(levels, 8))
        for g in range(8):
            far = levels[np.abs(levels - a[p, g]) >= 10]
            a[p, g + 8] = far[np.random.randint(len(far))]
    return np.exp2(a.ravel()).repeat(32)


BF16 = ml_dtypes.bfloat16


def bf(x):
    return np.asarray(x, np.float32).astype(BF16)


def f64(x):
    return np.asarray(x).astype(np.float64)


N, B, T, C, R, O, NC, H, W = 31, 128, 4, 256, 4, 512, 512, 16, 4
K = C * R
LEAKY_SLOPE = 0.01


def setup_inputs():
    s = mx_kscale(K)
    return {"pooled": bf((0.65 + 0.3 * np.random.standard_normal((N, B, K))) * s),
            "p": bf(0.65 + 0.5 * np.random.standard_normal((N, B, T, C))),
            "Wout": bf((4.0 / np.sqrt(K) * np.random.standard_normal((N, K, C)) - 4.0 / K) / s[None, :, None])}


def core(pooled, p, Wout):
    y = mxq(f64(pooled), 2, "e4m3") @ mxq(f64(Wout), 1, "e4m3")
    y = np.where(y >= 0, y, LEAKY_SLOPE * y)
    return np.max(f64(p) + y[:, :, None, :], axis=2)


def e4m3fn_bytes(y):
    return np.clip(np.asarray(y, np.float64), -448.0, 448.0).astype(np.float32).astype(ml_dtypes.float8_e4m3fn).view(np.uint8)


Y_SCALE = 120.0


def reference(pooled, p, Wout):
    out = core(pooled, p, Wout)
    return out, e4m3fn_bytes(out * Y_SCALE)

@@ -1,0 +1,225 @@
+from contextlib import ExitStack
+
+import concourse.mybir as mybir
+from concourse.masks import make_identity
+
+N_BINS, B, T, C, K = 31, 128, 4, 256, 1024
+FLOPS = 2 * N_BINS * B * K * C
+
+F32 = mybir.dt.float32
+BF16 = mybir.dt.bfloat16
+U32 = mybir.dt.uint32
+U8 = mybir.dt.uint8
+FP8X4 = mybir.dt.float8_e4m3fn_x4
+FP8 = mybir.dt.float8_e4m3fn
+ACT = mybir.ActivationFunctionType
+ALU = mybir.AluOpType
+
+P = 128
+SLOPE = 0.01
+Y_SCALE = 120.0
+MANUAL = True
+CV = 120
+PLAG = 2
+
+
+def tile_gmpahead_pa_kernel(tc, pooled, p, Wout, out_0, out_1):
+    nc = tc.nc
+    units = [(n0, min(2, N_BINS - n0)) for n0 in range(0, N_BINS, 2)]
+    U = len(units)
+
+    x_hbm = pooled.rearrange("n b k -> b n k")
+    p_hbm = p.rearrange("n b t c -> b n (t c)")
+    w_hbm = Wout.rearrange("n (g q j) c -> q (n g) (j c)", g=2, q=P, j=4)
+    o0_hbm = out_0.rearrange("n b c -> b n c")
+    o1_hbm = out_1.rearrange("n b c -> b n c")
+
+    with ExitStack() as ctx:
+        const = ctx.enter_context(tc.tile_pool(name="const", bufs=1))
+        raw = ctx.enter_context(tc.tile_pool(name="raw", bufs=4))
+        mid = ctx.enter_context(tc.tile_pool(name="mid", bufs=2))
+        epi = ctx.enter_context(tc.tile_pool(name="epi", bufs=3))
+        ps_t = ctx.enter_context(tc.psum_pool(name="ps_t", bufs=4))
+        ps_y = ctx.enter_context(tc.psum_pool(name="ps_y", bufs=3))
+
+        ident = const.tile([P, P], F32, name="ident")
+        make_identity(nc, ident[:])
+        warm = const.tile([P, 8], F32, name="warm")
+        warm2 = const.tile([P, 8], F32, name="warm2")
+        nc.vector.memset(warm[:], 0.0)
+        nc.scalar.activation(out=warm2[:], in_=warm[:], func=ACT.Copy, scale=1.0)
+
+        xraw, wraw, praw, xt, xg, xc, xs = {}, {}, {}, {}, {}, {}, {}
+        wg, wc, ws, yb, tt, uu, oo, f8, m2 = {}, {}, {}, {}, {}, {}, {}, {}, {}
+
+        def ok(s):
+            return 0 <= s < U
+
+        def load_x(s):
+            n0, nb = units[s]
+            xraw[s] = raw.tile([P, 2, K], BF16, name="xraw", tag="xraw")
+            nc.sync.dma_start(out=xraw[s][:, 0:nb, :], in_=x_hbm[:, n0:n0 + nb, :])
+
+        def load_w(s):
+            n0, nb = units[s]
+            wraw[s] = raw.tile([P, 4, K], BF16, name="wraw", tag="wraw")
+            nc.sync.dma_start(out=wraw[s][:, 0:2 * nb, :], in_=w_hbm[:, 2 * n0:2 * (n0 + nb), :])
+
+        def load_p(s):
+            n0, nb = units[s]
+            praw[s] = raw.tile([P, 2, T, C], BF16, name="praw", tag="praw")
+            nc.sync.dma_start(
+                out=praw[s][:, 0:nb].rearrange("b n t c -> b n (t c)"), in_=p_hbm[:, n0:n0 + nb, :]
+            )
+
+        def transposes(s):
+            n0, nb = units[s]
+            for i in range(nb):
+                words = xraw[s][:, i, :].bitcast(F32)
+                bank = ps_t.tile([P, 2, 2, B], F32, name="xt", tag="xt")
+                for g in range(2):
+                    for u in range(2):
+                        nc.tensor.transpose(bank[:, g, u, :], words[:, 256 * g + u:256 * (g + 1):2], ident[:])
+                xt[(s, i)] = bank
+
+        def evac(s):
+            n0, nb = units[s]
+            xg[s] = mid.tile([P, 2, 2, B, 4], BF16, name="xg", tag="xg", align_bytes=64)
+            for i in range(nb):
+                nc.scalar.copy(out=xg[s][:, i].bitcast(F32), in_=xt[(s, i)][:].rearrange("q g u b -> q g b u"))
+
+        def w_src(s, a0, a1, c0, c1):
+            return wraw[s][:, a0:a1, :].rearrange("q a (j c) -> q a c j", j=4)[:, :, c0:c1, :]
+
+        def inter_v(s):
+            n0, nb = units[s]
+            wg[s] = mid.tile([P, 4, C, 4], BF16, name="wg", tag="wg", align_bytes=64)
+            nc.vector.tensor_copy(out=wg[s][:, 0:2 * nb, 0:CV, :], in_=w_src(s, 0, 2 * nb, 0, CV))
+
+        def inter_s(s, i):
+            n0, nb = units[s]
+            if i < nb:
+                nc.scalar.copy(out=wg[s][:, 2 * i:2 * i + 2, CV:C, :], in_=w_src(s, 2 * i, 2 * i + 2, CV, C))
+
+        def quant_x(s):
+            n0, nb = units[s]
+            xc[s] = mid.tile([P, 2 * 2 * B], U32, name="xc", tag="xc", align_bytes=64)
+            xs[s] = mid.tile([P, 2 * 2 * B], U8, name="xs", tag="xs", align_bytes=64)
+            w = nb * 2 * B
+            nc.vector.quantize_mx(
+                out=xc[s][:, 0:w].bitcast(FP8X4),
+                scales=xs[s][:, 0:w],
+                in_=xg[s][:, 0:nb].rearrange("q n g b t -> q (n g b t)"),
+            )
+
+        def quant_w(s):
+            n0, nb = units[s]
+            wc[s] = mid.tile([P, 4 * C], U32, name="wc", tag="wc", align_bytes=64)
+            ws[s] = mid.tile([P, 4 * C], U8, name="ws", tag="ws", align_bytes=64)
+            for i in range(nb):
+                cols = slice(2 * i * C, (2 * i + 2) * C)
+                nc.vector.quantize_mx(
+                    out=wc[s][:, cols].bitcast(FP8X4),
+                    scales=ws[s][:, cols],
+                    in_=wg[s][:, 2 * i:2 * i + 2].rearrange("q a c j -> q (a c j)"),
+                )
+
+        def matmuls(s):
+            n0, nb = units[s]
+            yb[s] = ps_y.tile([P, 2 * C], F32, name="yb", tag="yb")
+            for i in range(nb):
+                for g in range(2):
+                    a = 2 * i + g
+                    nc.tensor.matmul_mx(
+                        out=yb[s][:, i * C:(i + 1) * C],
+                        lhsT=xc[s][:, a * B:(a + 1) * B].bitcast(FP8X4),
+                        lhsT_scale=xs[s][:, a * B:(a + 1) * B],
+                        rhs=wc[s][:, a * C:(a + 1) * C].bitcast(FP8X4),
+                        rhs_scale=ws[s][:, a * C:(a + 1) * C],
+                        start=(g == 0),
+                        stop=(g == 1),
+                    )
+
+        def slope(s):
+            n0, nb = units[s]
+            w = nb * C
+            tt[s] = epi.tile([P, 2 * C], F32, name="tt", tag="tt")
+            nc.scalar.activation(out=tt[s][:, 0:w], in_=yb[s][:, 0:w], func=ACT.Copy, scale=SLOPE)
+
+        def leaky(s):
+            n0, nb = units[s]
+            w = nb * C
+            uu[s] = epi.tile([P, 2 * C], F32, name="uu", tag="uu")
+            nc.vector.tensor_tensor(out=uu[s][:, 0:w], in0=yb[s][:, 0:w], in1=tt[s][:, 0:w], op=ALU.max)
+
+        def pmax(s):
+            n0, nb = units[s]
+            m1 = epi.tile([P, 2, 2, C], BF16, name="m1", tag="m1")
+            m2[s] = epi.tile([P, 2, C], BF16, name="m2", tag="m2")
+            nc.vector.tensor_tensor(
+                out=m1[:, 0:nb], in0=praw[s][:, 0:nb, 0:2, :], in1=praw[s][:, 0:nb, 2:4, :], op=ALU.max
+            )
+            nc.vector.tensor_tensor(out=m2[s][:, 0:nb], in0=m1[:, 0:nb, 0, :], in1=m1[:, 0:nb, 1, :], op=ALU.max)
+
+        def add_p(s):
+            n0, nb = units[s]
+            w = nb * C
+            oo[s] = epi.tile([P, 2 * C], F32, name="oo", tag="oo")
+            nc.vector.tensor_tensor(
+                out=oo[s][:, 0:w], in0=uu[s][:, 0:w], in1=m2[s][:, 0:nb].rearrange("b n c -> b (n c)"), op=ALU.add
+            )
+
+        def cast(s):
+            n0, nb = units[s]
+            w = nb * C
+            f8[s] = epi.tile([P, 2 * C], FP8, name="f8", tag="f8")
+            nc.scalar.activation(out=f8[s][:, 0:w], in_=oo[s][:, 0:w], func=ACT.Copy, scale=Y_SCALE, saturate=False)
+
+        def store(s):
+            n0, nb = units[s]
+            w = nb * C
+            nc.sync.dma_start(
+                out=o0_hbm[:, n0:n0 + nb, :], in_=oo[s][:, 0:w].rearrange("b (n c) -> b n c", n=nb)
+            )
+            nc.sync.dma_start(
+                out=o1_hbm[:, n0:n0 + nb, :],
+                in_=f8[s][:, 0:w].bitcast(U8).rearrange("b (n c) -> b n c", n=nb),
+            )
+
+        def body():
+            for s in range(-2, U + PLAG + 2):
+                if ok(s + 2):
+                    load_x(s + 2)
+                if ok(s + 1):
+                    load_w(s + 1)
+                if ok(s + 1 - PLAG):
+                    load_p(s + 1 - PLAG)
+                if ok(s - PLAG - 1):
+                    store(s - PLAG - 1)
+                if ok(s):
+                    inter_v(s)
+                    inter_s(s, 0)
+                if ok(s - 1):
+                    slope(s - 1)
+                if ok(s):
+                    inter_s(s, 1)
+                if ok(s - PLAG):
+                    pmax(s - PLAG)
+                if ok(s - 1):
+                    leaky(s - 1)
+                if ok(s - PLAG):
+                    add_p(s - PLAG)
+                    cast(s - PLAG)
+                if ok(s + 1):
+                    transposes(s + 1)
+                    evac(s + 1)
+                if ok(s):
+                    quant_x(s)
+                    quant_w(s)
+                    matmuls(s)
+
+        if MANUAL:
+            with tc.manual_schedule():
+                body()
+        else:
+            body()

@@ -19,8 +19,9 @@ P = 128
 SLOPE = 0.01
 Y_SCALE = 120.0
 MANUAL = True
-CV = 120
+CV = 112
 PLAG = 2
+SLAG = 6
 
 
 def tile_gmpahead_pa_kernel(tc, pooled, p, Wout, out_0, out_1):
@@ -28,7 +29,7 @@ def tile_gmpahead_pa_kernel(tc, pooled, p, Wout, out_0, out_1):
     units = [(n0, min(2, N_BINS - n0)) for n0 in range(0, N_BINS, 2)]
     U = len(units)
 
-    x_hbm = pooled.rearrange("n b k -> b n k")
+    x_rows = pooled.rearrange("n b k -> (n b) k")
     p_hbm = p.rearrange("n b t c -> b n (t c)")
     w_hbm = Wout.rearrange("n (g q j) c -> q (n g) (j c)", g=2, q=P, j=4)
     o0_hbm = out_0.rearrange("n b c -> b n c")
@@ -39,6 +40,7 @@ def tile_gmpahead_pa_kernel(tc, pooled, p, Wout, out_0, out_1):
         raw = ctx.enter_context(tc.tile_pool(name="raw", bufs=4))
         mid = ctx.enter_context(tc.tile_pool(name="mid", bufs=2))
         epi = ctx.enter_context(tc.tile_pool(name="epi", bufs=3))
+        late = ctx.enter_context(tc.tile_pool(name="late", bufs=SLAG - PLAG + 2))
         ps_t = ctx.enter_context(tc.psum_pool(name="ps_t", bufs=4))
         ps_y = ctx.enter_context(tc.psum_pool(name="ps_y", bufs=3))
 
@@ -58,7 +60,10 @@ def tile_gmpahead_pa_kernel(tc, pooled, p, Wout, out_0, out_1):
         def load_x(s):
             n0, nb = units[s]
             xraw[s] = raw.tile([P, 2, K], BF16, name="xraw", tag="xraw")
-            nc.sync.dma_start(out=xraw[s][:, 0:nb, :], in_=x_hbm[:, n0:n0 + nb, :])
+            nc.sync.dma_start(
+                out=xraw[s][:, 0:nb, :].rearrange("q e k -> q (e k)"),
+                in_=x_rows[n0 * B:(n0 + nb) * B, :].rearrange("(q e) k -> q (e k)", e=nb),
+            )
 
         def load_w(s):
             n0, nb = units[s]
@@ -74,19 +79,36 @@ def tile_gmpahead_pa_kernel(tc, pooled, p, Wout, out_0, out_1):
 
         def transposes(s):
             n0, nb = units[s]
-            for i in range(nb):
-                words = xraw[s][:, i, :].bitcast(F32)
+            if nb == 1:
+                words = xraw[s][:, 0, :].bitcast(F32)
                 bank = ps_t.tile([P, 2, 2, B], F32, name="xt", tag="xt")
                 for g in range(2):
                     for u in range(2):
                         nc.tensor.transpose(bank[:, g, u, :], words[:, 256 * g + u:256 * (g + 1):2], ident[:])
-                xt[(s, i)] = bank
+                xt[(s, 0)] = bank
+            else:
+                for g in range(2):
+                    bank = ps_t.tile([P, 2, 2, B], F32, name="xt", tag="xt")
+                    for u in range(2):
+                        for e in range(2):
+                            words = xraw[s][:, e, :].bitcast(F32)
+                            nc.tensor.transpose(bank[:, u, e, :], words[:, 256 * g + u:256 * (g + 1):2], ident[:])
+                    xt[(s, g)] = bank
 
         def evac(s):
             n0, nb = units[s]
-            xg[s] = mid.tile([P, 2, 2, B, 4], BF16, name="xg", tag="xg", align_bytes=64)
-            for i in range(nb):
-                nc.scalar.copy(out=xg[s][:, i].bitcast(F32), in_=xt[(s, i)][:].rearrange("q g u b -> q g b u"))
+            xg[s] = mid.tile([P, 2 * K], BF16, name="xg", tag="xg", align_bytes=64)
+            if nb == 1:
+                nc.scalar.copy(
+                    out=xg[s][:, 0:K].bitcast(F32).rearrange("p (g q u) -> p g q u", g=2, u=2),
+                    in_=xt[(s, 0)][:].rearrange("p g u q -> p g q u"),
+                )
+            else:
+                for g in range(2):
+                    nc.scalar.copy(
+                        out=xg[s][:, g * K:(g + 1) * K].bitcast(F32).rearrange("p (q e u) -> p q e u", e=2, u=2),
+                        in_=xt[(s, g)][:].rearrange("p u e q -> p q e u"),
+                    )
 
         def w_src(s, a0, a1, c0, c1):
             return wraw[s][:, a0:a1, :].rearrange("q a (j c) -> q a c j", j=4)[:, :, c0:c1, :]
@@ -109,20 +131,19 @@ def tile_gmpahead_pa_kernel(tc, pooled, p, Wout, out_0, out_1):
             nc.vector.quantize_mx(
                 out=xc[s][:, 0:w].bitcast(FP8X4),
                 scales=xs[s][:, 0:w],
-                in_=xg[s][:, 0:nb].rearrange("q n g b t -> q (n g b t)"),
+                in_=xg[s][:, 0:nb * K],
             )
 
         def quant_w(s):
             n0, nb = units[s]
             wc[s] = mid.tile([P, 4 * C], U32, name="wc", tag="wc", align_bytes=64)
             ws[s] = mid.tile([P, 4 * C], U8, name="ws", tag="ws", align_bytes=64)
-            for i in range(nb):
-                cols = slice(2 * i * C, (2 * i + 2) * C)
-                nc.vector.quantize_mx(
-                    out=wc[s][:, cols].bitcast(FP8X4),
-                    scales=ws[s][:, cols],
-                    in_=wg[s][:, 2 * i:2 * i + 2].rearrange("q a c j -> q (a c j)"),
-                )
+            w = 2 * nb * C
+            nc.vector.quantize_mx(
+                out=wc[s][:, 0:w].bitcast(FP8X4),
+                scales=ws[s][:, 0:w],
+                in_=wg[s][:, 0:2 * nb].rearrange("q a c j -> q (a c j)"),
+            )
 
         def matmuls(s):
             n0, nb = units[s]
@@ -130,10 +151,11 @@ def tile_gmpahead_pa_kernel(tc, pooled, p, Wout, out_0, out_1):
             for i in range(nb):
                 for g in range(2):
                     a = 2 * i + g
+                    x0 = (g * nb + i) * B
                     nc.tensor.matmul_mx(
                         out=yb[s][:, i * C:(i + 1) * C],
-                        lhsT=xc[s][:, a * B:(a + 1) * B].bitcast(FP8X4),
-                        lhsT_scale=xs[s][:, a * B:(a + 1) * B],
+                        lhsT=xc[s][:, x0:x0 + B].bitcast(FP8X4),
+                        lhsT_scale=xs[s][:, x0:x0 + B],
                         rhs=wc[s][:, a * C:(a + 1) * C].bitcast(FP8X4),
                         rhs_scale=ws[s][:, a * C:(a + 1) * C],
                         start=(g == 0),
@@ -149,7 +171,7 @@ def tile_gmpahead_pa_kernel(tc, pooled, p, Wout, out_0, out_1):
         def leaky(s):
             n0, nb = units[s]
             w = nb * C
-            uu[s] = epi.tile([P, 2 * C], F32, name="uu", tag="uu")
+            uu[s] = late.tile([P, 2 * C], F32, name="uu", tag="uu")
             nc.vector.tensor_tensor(out=uu[s][:, 0:w], in0=yb[s][:, 0:w], in1=tt[s][:, 0:w], op=ALU.max)
 
         def pmax(s):
@@ -164,7 +186,7 @@ def tile_gmpahead_pa_kernel(tc, pooled, p, Wout, out_0, out_1):
         def add_p(s):
             n0, nb = units[s]
             w = nb * C
-            oo[s] = epi.tile([P, 2 * C], F32, name="oo", tag="oo")
+            oo[s] = late.tile([P, 2 * C], F32, name="oo", tag="oo")
             nc.vector.tensor_tensor(
                 out=oo[s][:, 0:w], in0=uu[s][:, 0:w], in1=m2[s][:, 0:nb].rearrange("b n c -> b (n c)"), op=ALU.add
             )
@@ -172,7 +194,7 @@ def tile_gmpahead_pa_kernel(tc, pooled, p, Wout, out_0, out_1):
         def cast(s):
             n0, nb = units[s]
             w = nb * C
-            f8[s] = epi.tile([P, 2 * C], FP8, name="f8", tag="f8")
+            f8[s] = late.tile([P, 2 * C], FP8, name="f8", tag="f8")
             nc.scalar.activation(out=f8[s][:, 0:w], in_=oo[s][:, 0:w], func=ACT.Copy, scale=Y_SCALE, saturate=False)
 
         def store(s):
@@ -187,15 +209,15 @@ def tile_gmpahead_pa_kernel(tc, pooled, p, Wout, out_0, out_1):
             )
 
         def body():
-            for s in range(-2, U + PLAG + 2):
+            for s in range(-2, U + SLAG + 1):
                 if ok(s + 2):
                     load_x(s + 2)
                 if ok(s + 1):
                     load_w(s + 1)
                 if ok(s + 1 - PLAG):
                     load_p(s + 1 - PLAG)
-                if ok(s - PLAG - 1):
-                    store(s - PLAG - 1)
+                if ok(s - SLAG):
+                    store(s - SLAG)
                 if ok(s):
                     inter_v(s)
                     inter_s(s, 0)

@@ -21,12 +21,14 @@ Y_SCALE = 120.0
 MANUAL = True
 CV = 112
 PLAG = 2
-SLAG = 6
+SLAG = 5
 
 
 def tile_gmpahead_pa_kernel(tc, pooled, p, Wout, out_0, out_1):
     nc = tc.nc
-    units = [(n0, min(2, N_BINS - n0)) for n0 in range(0, N_BINS, 2)]
+    sizes = [2] * 15 + [1]
+    assert sum(sizes) == N_BINS
+    units = [(sum(sizes[0:i]), sizes[i]) for i in range(len(sizes))]
     U = len(units)
 
     x_rows = pooled.rearrange("n b k -> (n b) k")
@@ -52,7 +54,7 @@ def tile_gmpahead_pa_kernel(tc, pooled, p, Wout, out_0, out_1):
         nc.scalar.activation(out=warm2[:], in_=warm[:], func=ACT.Copy, scale=1.0)
 
         xraw, wraw, praw, xt, xg, xc, xs = {}, {}, {}, {}, {}, {}, {}
-        wg, wc, ws, yb, tt, uu, oo, f8, m2 = {}, {}, {}, {}, {}, {}, {}, {}, {}
+        wg, wc, ws, yb, tt, uu, oo, f8, m1, m2 = {}, {}, {}, {}, {}, {}, {}, {}, {}, {}
 
         def ok(s):
             return 0 <= s < U
@@ -138,12 +140,13 @@ def tile_gmpahead_pa_kernel(tc, pooled, p, Wout, out_0, out_1):
             n0, nb = units[s]
             wc[s] = mid.tile([P, 4 * C], U32, name="wc", tag="wc", align_bytes=64)
             ws[s] = mid.tile([P, 4 * C], U8, name="ws", tag="ws", align_bytes=64)
-            w = 2 * nb * C
-            nc.vector.quantize_mx(
-                out=wc[s][:, 0:w].bitcast(FP8X4),
-                scales=ws[s][:, 0:w],
-                in_=wg[s][:, 0:2 * nb].rearrange("q a c j -> q (a c j)"),
-            )
+            for i in range(nb):
+                cols = slice(2 * i * C, (2 * i + 2) * C)
+                nc.vector.quantize_mx(
+                    out=wc[s][:, cols].bitcast(FP8X4),
+                    scales=ws[s][:, cols],
+                    in_=wg[s][:, 2 * i:2 * i + 2].rearrange("q a c j -> q (a c j)"),
+                )
 
         def matmuls(s):
             n0, nb = units[s]
@@ -174,14 +177,19 @@ def tile_gmpahead_pa_kernel(tc, pooled, p, Wout, out_0, out_1):
             uu[s] = late.tile([P, 2 * C], F32, name="uu", tag="uu")
             nc.vector.tensor_tensor(out=uu[s][:, 0:w], in0=yb[s][:, 0:w], in1=tt[s][:, 0:w], op=ALU.max)
 
-        def pmax(s):
+        def pmax1(s):
             n0, nb = units[s]
-            m1 = epi.tile([P, 2, 2, C], BF16, name="m1", tag="m1")
+            m1[s] = epi.tile([P, 2, 2, C], BF16, name="m1", tag="m1")
+            nc.vector.tensor_tensor(
+                out=m1[s][:, 0:nb], in0=praw[s][:, 0:nb, 0:2, :], in1=praw[s][:, 0:nb, 2:4, :], op=ALU.max
+            )
+
+        def pmax2(s):
+            n0, nb = units[s]
             m2[s] = epi.tile([P, 2, C], BF16, name="m2", tag="m2")
             nc.vector.tensor_tensor(
-                out=m1[:, 0:nb], in0=praw[s][:, 0:nb, 0:2, :], in1=praw[s][:, 0:nb, 2:4, :], op=ALU.max
+                out=m2[s][:, 0:nb], in0=m1[s][:, 0:nb, 0, :], in1=m1[s][:, 0:nb, 1, :], op=ALU.max
             )
-            nc.vector.tensor_tensor(out=m2[s][:, 0:nb], in0=m1[:, 0:nb, 0, :], in1=m1[:, 0:nb, 1, :], op=ALU.max)
 
         def add_p(s):
             n0, nb = units[s]
@@ -226,17 +234,20 @@ def tile_gmpahead_pa_kernel(tc, pooled, p, Wout, out_0, out_1):
                 if ok(s):
                     inter_s(s, 1)
                 if ok(s - PLAG):
-                    pmax(s - PLAG)
+                    pmax1(s - PLAG)
                 if ok(s - 1):
                     leaky(s - 1)
                 if ok(s - PLAG):
-                    add_p(s - PLAG)
-                    cast(s - PLAG)
+                    pmax2(s - PLAG)
                 if ok(s + 1):
                     transposes(s + 1)
                     evac(s + 1)
                 if ok(s):
                     quant_x(s)
+                if ok(s - PLAG):
+                    add_p(s - PLAG)
+                    cast(s - PLAG)
+                if ok(s):
                     quant_w(s)
                     matmuls(s)
 

@@ -21,7 +21,7 @@ Y_SCALE = 120.0
 MANUAL = True
 CV = 112
 PLAG = 2
-SLAG = 5
+SLAG = 7
 
 
 def tile_gmpahead_pa_kernel(tc, pooled, p, Wout, out_0, out_1):
@@ -113,17 +113,20 @@ def tile_gmpahead_pa_kernel(tc, pooled, p, Wout, out_0, out_1):
                     )
 
         def w_src(s, a0, a1, c0, c1):
-            return wraw[s][:, a0:a1, :].rearrange("q a (j c) -> q a c j", j=4)[:, :, c0:c1, :]
+            return wraw[s][:, a0:a1, :].rearrange("q a (j c i) -> q a c j i", j=4, i=4)[:, :, c0 // 4:c1 // 4, :, :]
+
+        def w_dst(s, a0, a1, c0, c1):
+            return wg[s][:, a0:a1].rearrange("q a (c i) j -> q a c j i", i=4)[:, :, c0 // 4:c1 // 4, :, :]
 
         def inter_v(s):
             n0, nb = units[s]
             wg[s] = mid.tile([P, 4, C, 4], BF16, name="wg", tag="wg", align_bytes=64)
-            nc.vector.tensor_copy(out=wg[s][:, 0:2 * nb, 0:CV, :], in_=w_src(s, 0, 2 * nb, 0, CV))
+            nc.vector.tensor_copy(out=w_dst(s, 0, 2 * nb, 0, CV), in_=w_src(s, 0, 2 * nb, 0, CV))
 
         def inter_s(s, i):
             n0, nb = units[s]
             if i < nb:
-                nc.scalar.copy(out=wg[s][:, 2 * i:2 * i + 2, CV:C, :], in_=w_src(s, 2 * i, 2 * i + 2, CV, C))
+                nc.scalar.copy(out=w_dst(s, 2 * i, 2 * i + 2, CV, C), in_=w_src(s, 2 * i, 2 * i + 2, CV, C))
 
         def quant_x(s):
             n0, nb = units[s]

@@ -20,7 +20,8 @@ SLOPE = 0.01
 Y_SCALE = 120.0
 MANUAL = True
 CV = 112
-PLAG = 2
+CV_EDGE = 176
+PLAG = 1
 SLAG = 7
 
 
@@ -58,6 +59,9 @@ def tile_gmpahead_pa_kernel(tc, pooled, p, Wout, out_0, out_1):
 
         def ok(s):
             return 0 <= s < U
+
+        def cv_of(s):
+            return CV_EDGE if s in (0, U - 1) else CV
 
         def load_x(s):
             n0, nb = units[s]
@@ -121,12 +125,12 @@ def tile_gmpahead_pa_kernel(tc, pooled, p, Wout, out_0, out_1):
         def inter_v(s):
             n0, nb = units[s]
             wg[s] = mid.tile([P, 4, C, 4], BF16, name="wg", tag="wg", align_bytes=64)
-            nc.vector.tensor_copy(out=w_dst(s, 0, 2 * nb, 0, CV), in_=w_src(s, 0, 2 * nb, 0, CV))
+            nc.vector.tensor_copy(out=w_dst(s, 0, 2 * nb, 0, cv_of(s)), in_=w_src(s, 0, 2 * nb, 0, cv_of(s)))
 
         def inter_s(s, i):
             n0, nb = units[s]
             if i < nb:
-                nc.scalar.copy(out=w_dst(s, 2 * i, 2 * i + 2, CV, C), in_=w_src(s, 2 * i, 2 * i + 2, CV, C))
+                nc.scalar.copy(out=w_dst(s, 2 * i, 2 * i + 2, cv_of(s), C), in_=w_src(s, 2 * i, 2 * i + 2, cv_of(s), C))
 
         def quant_x(s):
             n0, nb = units[s]
@@ -221,9 +225,8 @@ def tile_gmpahead_pa_kernel(tc, pooled, p, Wout, out_0, out_1):
 
         def body():
             for s in range(-2, U + SLAG + 1):
-                if ok(s + 2):
-                    load_x(s + 2)
                 if ok(s + 1):
+                    load_x(s + 1)
                     load_w(s + 1)
                 if ok(s + 1 - PLAG):
                     load_p(s + 1 - PLAG)

@@ -10,6 +10,7 @@ F32 = mybir.dt.float32
 BF16 = mybir.dt.bfloat16
 U32 = mybir.dt.uint32
 U8 = mybir.dt.uint8
+I32 = mybir.dt.int32
 FP8X4 = mybir.dt.float8_e4m3fn_x4
 FP8 = mybir.dt.float8_e4m3fn
 ACT = mybir.ActivationFunctionType
@@ -21,8 +22,11 @@ Y_SCALE = 120.0
 MANUAL = True
 CV = 112
 CV_EDGE = 176
-PLAG = 1
-SLAG = 7
+QLAG = 0
+LLAG = 2
+PLAG = 2
+SLAG = 8
+WG_BUFS = 2
 
 
 def tile_gmpahead_pa_kernel(tc, pooled, p, Wout, out_0, out_1):
@@ -33,15 +37,16 @@ def tile_gmpahead_pa_kernel(tc, pooled, p, Wout, out_0, out_1):
     U = len(units)
 
     x_rows = pooled.rearrange("n b k -> (n b) k")
-    p_hbm = p.rearrange("n b t c -> b n (t c)")
+    p_rows = p.rearrange("n b t c -> (n b) (t c)")
     w_hbm = Wout.rearrange("n (g q j) c -> q (n g) (j c)", g=2, q=P, j=4)
-    o0_hbm = out_0.rearrange("n b c -> b n c")
-    o1_hbm = out_1.rearrange("n b c -> b n c")
+    o0_rows = out_0.rearrange("n b c -> (n b) c")
+    o1_rows = out_1.rearrange("n b c -> (n b) c")
 
     with ExitStack() as ctx:
         const = ctx.enter_context(tc.tile_pool(name="const", bufs=1))
         raw = ctx.enter_context(tc.tile_pool(name="raw", bufs=4))
         mid = ctx.enter_context(tc.tile_pool(name="mid", bufs=2))
+        wgp = ctx.enter_context(tc.tile_pool(name="wgp", bufs=WG_BUFS))
         epi = ctx.enter_context(tc.tile_pool(name="epi", bufs=3))
         late = ctx.enter_context(tc.tile_pool(name="late", bufs=SLAG - PLAG + 2))
         ps_t = ctx.enter_context(tc.psum_pool(name="ps_t", bufs=4))
@@ -53,6 +58,16 @@ def tile_gmpahead_pa_kernel(tc, pooled, p, Wout, out_0, out_1):
         warm2 = const.tile([P, 8], F32, name="warm2")
         nc.vector.memset(warm[:], 0.0)
         nc.scalar.activation(out=warm2[:], in_=warm[:], func=ACT.Copy, scale=1.0)
+
+        H = B // 2
+        xc_keep, xs_keep = [], []
+        for r in range(2):
+            xc_r = const.tile([P, 12 * H], U32, name="xc%d" % r, align_bytes=64)
+            xs_r = const.tile([P, 12 * H], U8, name="xs%d" % r, align_bytes=64)
+            nc.vector.memset(xc_r[:].bitcast(I32), 0)
+            nc.vector.memset(xs_r[:].bitcast(I32), 0)
+            xc_keep.append(xc_r)
+            xs_keep.append(xs_r)
 
         xraw, wraw, praw, xt, xg, xc, xs = {}, {}, {}, {}, {}, {}, {}
         wg, wc, ws, yb, tt, uu, oo, f8, m1, m2 = {}, {}, {}, {}, {}, {}, {}, {}, {}, {}
@@ -80,7 +95,8 @@ def tile_gmpahead_pa_kernel(tc, pooled, p, Wout, out_0, out_1):
             n0, nb = units[s]
             praw[s] = raw.tile([P, 2, T, C], BF16, name="praw", tag="praw")
             nc.sync.dma_start(
-                out=praw[s][:, 0:nb].rearrange("b n t c -> b n (t c)"), in_=p_hbm[:, n0:n0 + nb, :]
+                out=praw[s][:, 0:nb].rearrange("q e t c -> q (e t c)"),
+                in_=p_rows[n0 * B:(n0 + nb) * B, :].rearrange("(q e) f -> q (e f)", e=nb),
             )
 
         def transposes(s):
@@ -112,8 +128,8 @@ def tile_gmpahead_pa_kernel(tc, pooled, p, Wout, out_0, out_1):
             else:
                 for g in range(2):
                     nc.scalar.copy(
-                        out=xg[s][:, g * K:(g + 1) * K].bitcast(F32).rearrange("p (q e u) -> p q e u", e=2, u=2),
-                        in_=xt[(s, g)][:].rearrange("p u e q -> p q e u"),
+                        out=xg[s][:, g * K:(g + 1) * K].bitcast(F32).rearrange("p (e q u) -> p e q u", e=2, u=2),
+                        in_=xt[(s, g)][:].rearrange("p u e q -> p e q u"),
                     )
 
         def w_src(s, a0, a1, c0, c1):
@@ -124,7 +140,7 @@ def tile_gmpahead_pa_kernel(tc, pooled, p, Wout, out_0, out_1):
 
         def inter_v(s):
             n0, nb = units[s]
-            wg[s] = mid.tile([P, 4, C, 4], BF16, name="wg", tag="wg", align_bytes=64)
+            wg[s] = wgp.tile([P, 4, C, 4], BF16, name="wg", tag="wg", align_bytes=64)
             nc.vector.tensor_copy(out=w_dst(s, 0, 2 * nb, 0, cv_of(s)), in_=w_src(s, 0, 2 * nb, 0, cv_of(s)))
 
         def inter_s(s, i):
@@ -134,14 +150,20 @@ def tile_gmpahead_pa_kernel(tc, pooled, p, Wout, out_0, out_1):
 
         def quant_x(s):
             n0, nb = units[s]
-            xc[s] = mid.tile([P, 2 * 2 * B], U32, name="xc", tag="xc", align_bytes=64)
-            xs[s] = mid.tile([P, 2 * 2 * B], U8, name="xs", tag="xs", align_bytes=64)
-            w = nb * 2 * B
-            nc.vector.quantize_mx(
-                out=xc[s][:, 0:w].bitcast(FP8X4),
-                scales=xs[s][:, 0:w],
-                in_=xg[s][:, 0:nb * K],
-            )
+            if nb == 1:
+                xc[s] = mid.tile([P, 2 * B], U32, name="xc", tag="xc", align_bytes=64)
+                xs[s] = mid.tile([P, 2 * B], U8, name="xs", tag="xs", align_bytes=64)
+                nc.vector.quantize_mx(out=xc[s][:].bitcast(FP8X4), scales=xs[s][:], in_=xg[s][:, 0:K])
+                return
+            xc[s] = xc_keep[s % 2]
+            xs[s] = xs_keep[s % 2]
+            runs = [(0, 1, 0)] + [(2 * r - 1, 2, 3 * r - 1) for r in (1, 2, 3)] + [(7, 1, 11)]
+            for src, n, dst in runs:
+                nc.vector.quantize_mx(
+                    out=xc[s][:, dst * H:(dst + n) * H].bitcast(FP8X4),
+                    scales=xs[s][:, dst * H:(dst + n) * H],
+                    in_=xg[s][:, src * 4 * H:(src + n) * 4 * H],
+                )
 
         def quant_w(s):
             n0, nb = units[s]
@@ -158,19 +180,32 @@ def tile_gmpahead_pa_kernel(tc, pooled, p, Wout, out_0, out_1):
         def matmuls(s):
             n0, nb = units[s]
             yb[s] = ps_y.tile([P, 2 * C], F32, name="yb", tag="yb")
-            for i in range(nb):
+            if nb == 1:
                 for g in range(2):
-                    a = 2 * i + g
-                    x0 = (g * nb + i) * B
                     nc.tensor.matmul_mx(
-                        out=yb[s][:, i * C:(i + 1) * C],
-                        lhsT=xc[s][:, x0:x0 + B].bitcast(FP8X4),
-                        lhsT_scale=xs[s][:, x0:x0 + B],
-                        rhs=wc[s][:, a * C:(a + 1) * C].bitcast(FP8X4),
-                        rhs_scale=ws[s][:, a * C:(a + 1) * C],
+                        out=yb[s][:, 0:C],
+                        lhsT=xc[s][:, g * B:(g + 1) * B].bitcast(FP8X4),
+                        lhsT_scale=xs[s][:, g * B:(g + 1) * B],
+                        rhs=wc[s][:, g * C:(g + 1) * C].bitcast(FP8X4),
+                        rhs_scale=ws[s][:, g * C:(g + 1) * C],
                         start=(g == 0),
                         stop=(g == 1),
                     )
+                return
+            for e in range(2):
+                for i in range(2):
+                    for g in range(2):
+                        a = 2 * i + g
+                        x0 = (3 * (2 * g + e) + i) * H
+                        nc.tensor.matmul_mx(
+                            out=yb[s][:, e * C:(e + 1) * C],
+                            lhsT=xc[s][:, x0:x0 + B].bitcast(FP8X4),
+                            lhsT_scale=xs[s][:, x0:x0 + B],
+                            rhs=wc[s][:, a * C:(a + 1) * C].bitcast(FP8X4),
+                            rhs_scale=ws[s][:, a * C:(a + 1) * C],
+                            start=(i == 0 and g == 0),
+                            stop=(i == 1 and g == 1),
+                        )
 
         def slope(s):
             n0, nb = units[s]
@@ -216,11 +251,11 @@ def tile_gmpahead_pa_kernel(tc, pooled, p, Wout, out_0, out_1):
             n0, nb = units[s]
             w = nb * C
             nc.sync.dma_start(
-                out=o0_hbm[:, n0:n0 + nb, :], in_=oo[s][:, 0:w].rearrange("b (n c) -> b n c", n=nb)
+                out=o0_rows[n0 * B:(n0 + nb) * B, :].rearrange("(q e) c -> q (e c)", e=nb), in_=oo[s][:, 0:w]
             )
             nc.sync.dma_start(
-                out=o1_hbm[:, n0:n0 + nb, :],
-                in_=f8[s][:, 0:w].bitcast(U8).rearrange("b (n c) -> b n c", n=nb),
+                out=o1_rows[n0 * B:(n0 + nb) * B, :].rearrange("(q e) c -> q (e c)", e=nb),
+                in_=f8[s][:, 0:w].bitcast(U8),
             )
 
         def body():
@@ -235,27 +270,27 @@ def tile_gmpahead_pa_kernel(tc, pooled, p, Wout, out_0, out_1):
                 if ok(s):
                     inter_v(s)
                     inter_s(s, 0)
-                if ok(s - 1):
-                    slope(s - 1)
+                if ok(s - LLAG):
+                    slope(s - LLAG)
                 if ok(s):
                     inter_s(s, 1)
                 if ok(s - PLAG):
                     pmax1(s - PLAG)
-                if ok(s - 1):
-                    leaky(s - 1)
+                if ok(s - LLAG):
+                    leaky(s - LLAG)
                 if ok(s - PLAG):
                     pmax2(s - PLAG)
-                if ok(s + 1):
-                    transposes(s + 1)
-                    evac(s + 1)
-                if ok(s):
-                    quant_x(s)
+                if ok(s + 1 - QLAG):
+                    transposes(s + 1 - QLAG)
+                    evac(s + 1 - QLAG)
+                if ok(s - QLAG):
+                    quant_x(s - QLAG)
                 if ok(s - PLAG):
                     add_p(s - PLAG)
                     cast(s - PLAG)
-                if ok(s):
-                    quant_w(s)
-                    matmuls(s)
+                if ok(s - QLAG):
+                    quant_w(s - QLAG)
+                    matmuls(s - QLAG)
 
         if MANUAL:
             with tc.manual_schedule():

@@ -36,6 +36,10 @@ def tile_gmpahead_pa_kernel(tc, pooled, p, Wout, out_0, out_1):
     units = [(sum(sizes[0:i]), sizes[i]) for i in range(len(sizes))]
     U = len(units)
 
+    x_groups = [[0], [1], [2], [3]] + [[u, u + 1] for u in range(4, 14, 2)] + [[14], [15]]
+    p_groups = x_groups
+    po_groups = [[u, u + 1] for u in range(0, 14, 2)] + [[14], [15]]
+
     x_rows = pooled.rearrange("n b k -> (n b) k")
     p_rows = p.rearrange("n b t c -> (n b) (t c)")
     w_hbm = Wout.rearrange("n (g q j) c -> q (n g) (j c)", g=2, q=P, j=4)
@@ -48,7 +52,7 @@ def tile_gmpahead_pa_kernel(tc, pooled, p, Wout, out_0, out_1):
         mid = ctx.enter_context(tc.tile_pool(name="mid", bufs=2))
         wgp = ctx.enter_context(tc.tile_pool(name="wgp", bufs=WG_BUFS))
         epi = ctx.enter_context(tc.tile_pool(name="epi", bufs=3))
-        late = ctx.enter_context(tc.tile_pool(name="late", bufs=SLAG - PLAG + 2))
+        late = ctx.enter_context(tc.tile_pool(name="late", bufs=(SLAG - PLAG) // 2 + 3))
         ps_t = ctx.enter_context(tc.psum_pool(name="ps_t", bufs=4))
         ps_y = ctx.enter_context(tc.psum_pool(name="ps_y", bufs=3))
 
@@ -71,6 +75,7 @@ def tile_gmpahead_pa_kernel(tc, pooled, p, Wout, out_0, out_1):
 
         xraw, wraw, praw, xt, xg, xc, xs = {}, {}, {}, {}, {}, {}, {}
         wg, wc, ws, yb, tt, uu, oo, f8, m1, m2 = {}, {}, {}, {}, {}, {}, {}, {}, {}, {}
+        oo_both, f8_both = {}, {}
 
         def ok(s):
             return 0 <= s < U
@@ -78,13 +83,24 @@ def tile_gmpahead_pa_kernel(tc, pooled, p, Wout, out_0, out_1):
         def cv_of(s):
             return CV_EDGE if s in (0, U - 1) else CV
 
+        def group_of(groups, s):
+            return [grp for grp in groups if s in grp][0]
+
+        def rows_of(rows, grp):
+            n0, nb = units[grp[0]]
+            return rows[n0 * B:(n0 + nb * len(grp)) * B, :].rearrange("(j q e) f -> q j (e f)", j=len(grp), e=nb)
+
         def load_x(s):
+            grp = group_of(x_groups, s)
+            if s != grp[0]:
+                return
             n0, nb = units[s]
-            xraw[s] = raw.tile([P, 2, K], BF16, name="xraw", tag="xraw")
+            both = raw.tile([P, 2, 2, K], BF16, name="xraw", tag="xraw")
             nc.sync.dma_start(
-                out=xraw[s][:, 0:nb, :].rearrange("q e k -> q (e k)"),
-                in_=x_rows[n0 * B:(n0 + nb) * B, :].rearrange("(q e) k -> q (e k)", e=nb),
+                out=both[:, 0:len(grp), 0:nb, :].rearrange("q j e k -> q j (e k)"), in_=rows_of(x_rows, grp)
             )
+            for j in range(len(grp)):
+                xraw[grp[j]] = both[:, j]
 
         def load_w(s):
             n0, nb = units[s]
@@ -92,12 +108,16 @@ def tile_gmpahead_pa_kernel(tc, pooled, p, Wout, out_0, out_1):
             nc.sync.dma_start(out=wraw[s][:, 0:2 * nb, :], in_=w_hbm[:, 2 * n0:2 * (n0 + nb), :])
 
         def load_p(s):
+            grp = group_of(p_groups, s)
+            if s != grp[0]:
+                return
             n0, nb = units[s]
-            praw[s] = raw.tile([P, 2, T, C], BF16, name="praw", tag="praw")
+            both = raw.tile([P, 2, 2, T, C], BF16, name="praw", tag="praw")
             nc.sync.dma_start(
-                out=praw[s][:, 0:nb].rearrange("q e t c -> q (e t c)"),
-                in_=p_rows[n0 * B:(n0 + nb) * B, :].rearrange("(q e) f -> q (e f)", e=nb),
+                out=both[:, 0:len(grp), 0:nb].rearrange("q j e t c -> q j (e t c)"), in_=rows_of(p_rows, grp)
             )
+            for j in range(len(grp)):
+                praw[grp[j]] = both[:, j]
 
         def transposes(s):
             n0, nb = units[s]
@@ -216,7 +236,7 @@ def tile_gmpahead_pa_kernel(tc, pooled, p, Wout, out_0, out_1):
         def leaky(s):
             n0, nb = units[s]
             w = nb * C
-            uu[s] = late.tile([P, 2 * C], F32, name="uu", tag="uu")
+            uu[s] = epi.tile([P, 2 * C], F32, name="uu", tag="uu")
             nc.vector.tensor_tensor(out=uu[s][:, 0:w], in0=yb[s][:, 0:w], in1=tt[s][:, 0:w], op=ALU.max)
 
         def pmax1(s):
@@ -236,7 +256,11 @@ def tile_gmpahead_pa_kernel(tc, pooled, p, Wout, out_0, out_1):
         def add_p(s):
             n0, nb = units[s]
             w = nb * C
-            oo[s] = late.tile([P, 2 * C], F32, name="oo", tag="oo")
+            grp = group_of(po_groups, s)
+            if s == grp[0]:
+                oo_both[s] = late.tile([P, 2, 2 * C], F32, name="oo", tag="oo")
+                for j in range(len(grp)):
+                    oo[grp[j]] = oo_both[s][:, j]
             nc.vector.tensor_tensor(
                 out=oo[s][:, 0:w], in0=uu[s][:, 0:w], in1=m2[s][:, 0:nb].rearrange("b n c -> b (n c)"), op=ALU.add
             )
@@ -244,19 +268,21 @@ def tile_gmpahead_pa_kernel(tc, pooled, p, Wout, out_0, out_1):
         def cast(s):
             n0, nb = units[s]
             w = nb * C
-            f8[s] = late.tile([P, 2 * C], FP8, name="f8", tag="f8")
+            grp = group_of(po_groups, s)
+            if s == grp[0]:
+                f8_both[s] = late.tile([P, 2, 2 * C], FP8, name="f8", tag="f8")
+                for j in range(len(grp)):
+                    f8[grp[j]] = f8_both[s][:, j]
             nc.scalar.activation(out=f8[s][:, 0:w], in_=oo[s][:, 0:w], func=ACT.Copy, scale=Y_SCALE, saturate=False)
 
         def store(s):
+            grp = group_of(po_groups, s)
+            if s != grp[-1]:
+                return
             n0, nb = units[s]
             w = nb * C
-            nc.sync.dma_start(
-                out=o0_rows[n0 * B:(n0 + nb) * B, :].rearrange("(q e) c -> q (e c)", e=nb), in_=oo[s][:, 0:w]
-            )
-            nc.sync.dma_start(
-                out=o1_rows[n0 * B:(n0 + nb) * B, :].rearrange("(q e) c -> q (e c)", e=nb),
-                in_=f8[s][:, 0:w].bitcast(U8),
-            )
+            nc.sync.dma_start(out=rows_of(o0_rows, grp), in_=oo_both[grp[0]][:, 0:len(grp), 0:w])
+            nc.sync.dma_start(out=rows_of(o1_rows, grp), in_=f8_both[grp[0]][:, 0:len(grp), 0:w].bitcast(U8))
 
         def body():
             for s in range(-2, U + SLAG + 1):

@@ -36,7 +36,7 @@ def tile_gmpahead_pa_kernel(tc, pooled, p, Wout, out_0, out_1):
     units = [(sum(sizes[0:i]), sizes[i]) for i in range(len(sizes))]
     U = len(units)
 
-    x_groups = [[0], [1], [2], [3]] + [[u, u + 1] for u in range(4, 14, 2)] + [[14], [15]]
+    x_groups = [[u] for u in range(16)]
     p_groups = x_groups
     po_groups = [[u, u + 1] for u in range(0, 14, 2)] + [[14], [15]]
 

@@ -22,6 +22,8 @@ Y_SCALE = 120.0
 MANUAL = True
 CV = 112
 CV_EDGE = 176
+CV_LAST = 48
+CV_LATE = 80
 QLAG = 0
 LLAG = 2
 PLAG = 2
@@ -81,7 +83,7 @@ def tile_gmpahead_pa_kernel(tc, pooled, p, Wout, out_0, out_1):
             return 0 <= s < U
 
         def cv_of(s):
-            return CV_EDGE if s in (0, U - 1) else CV
+            return CV_EDGE if s == 0 else CV_LAST if s == U - 1 else CV_LATE if s == U - 2 else CV
 
         def group_of(groups, s):
             return [grp for grp in groups if s in grp][0]
@@ -293,11 +295,11 @@ def tile_gmpahead_pa_kernel(tc, pooled, p, Wout, out_0, out_1):
                     load_p(s + 1 - PLAG)
                 if ok(s - SLAG):
                     store(s - SLAG)
+                if ok(s - LLAG):
+                    slope(s - LLAG)
                 if ok(s):
                     inter_v(s)
                     inter_s(s, 0)
-                if ok(s - LLAG):
-                    slope(s - LLAG)
                 if ok(s):
                     inter_s(s, 1)
                 if ok(s - PLAG):

from contextlib import ExitStack

import concourse.mybir as mybir
from concourse.masks import make_identity

N_BINS, B, T, C, K = 31, 128, 4, 256, 1024
FLOPS = 2 * N_BINS * B * K * C

F32 = mybir.dt.float32
BF16 = mybir.dt.bfloat16
U32 = mybir.dt.uint32
U8 = mybir.dt.uint8
I32 = mybir.dt.int32
FP8X4 = mybir.dt.float8_e4m3fn_x4
FP8 = mybir.dt.float8_e4m3fn
ACT = mybir.ActivationFunctionType
ALU = mybir.AluOpType

P = 128
SLOPE = 0.01
Y_SCALE = 120.0
MANUAL = True
CV = 112
CV_EDGE = 176
CV_LAST = 48
CV_LATE = 80
QLAG = 0
LLAG = 2
PLAG = 2
SLAG = 8
WG_BUFS = 2


def tile_gmpahead_pa_kernel(tc, pooled, p, Wout, out_0, out_1):
    nc = tc.nc
    sizes = [2] * 15 + [1]
    assert sum(sizes) == N_BINS
    units = [(sum(sizes[0:i]), sizes[i]) for i in range(len(sizes))]
    U = len(units)

    x_groups = [[u] for u in range(16)]
    p_groups = x_groups
    po_groups = [[u, u + 1] for u in range(0, 14, 2)] + [[14], [15]]

    x_rows = pooled.rearrange("n b k -> (n b) k")
    p_rows = p.rearrange("n b t c -> (n b) (t c)")
    w_hbm = Wout.rearrange("n (g q j) c -> q (n g) (j c)", g=2, q=P, j=4)
    o0_rows = out_0.rearrange("n b c -> (n b) c")
    o1_rows = out_1.rearrange("n b c -> (n b) c")

    with ExitStack() as ctx:
        const = ctx.enter_context(tc.tile_pool(name="const", bufs=1))
        raw = ctx.enter_context(tc.tile_pool(name="raw", bufs=4))
        mid = ctx.enter_context(tc.tile_pool(name="mid", bufs=2))
        wgp = ctx.enter_context(tc.tile_pool(name="wgp", bufs=WG_BUFS))
        epi = ctx.enter_context(tc.tile_pool(name="epi", bufs=3))
        late = ctx.enter_context(tc.tile_pool(name="late", bufs=(SLAG - PLAG) // 2 + 3))
        ps_t = ctx.enter_context(tc.psum_pool(name="ps_t", bufs=4))
        ps_y = ctx.enter_context(tc.psum_pool(name="ps_y", bufs=3))

        ident = const.tile([P, P], F32, name="ident")
        make_identity(nc, ident[:])
        warm = const.tile([P, 8], F32, name="warm")
        warm2 = const.tile([P, 8], F32, name="warm2")
        nc.vector.memset(warm[:], 0.0)
        nc.scalar.activation(out=warm2[:], in_=warm[:], func=ACT.Copy, scale=1.0)

        H = B // 2
        xc_keep, xs_keep = [], []
        for r in range(2):
            xc_r = const.tile([P, 12 * H], U32, name="xc%d" % r, align_bytes=64)
            xs_r = const.tile([P, 12 * H], U8, name="xs%d" % r, align_bytes=64)
            nc.vector.memset(xc_r[:].bitcast(I32), 0)
            nc.vector.memset(xs_r[:].bitcast(I32), 0)
            xc_keep.append(xc_r)
            xs_keep.append(xs_r)

        xraw, wraw, praw, xt, xg, xc, xs = {}, {}, {}, {}, {}, {}, {}
        wg, wc, ws, yb, tt, uu, oo, f8, m1, m2 = {}, {}, {}, {}, {}, {}, {}, {}, {}, {}
        oo_both, f8_both = {}, {}

        def ok(s):
            return 0 <= s < U

        def cv_of(s):
            return CV_EDGE if s == 0 else CV_LAST if s == U - 1 else CV_LATE if s == U - 2 else CV

        def group_of(groups, s):
            return [grp for grp in groups if s in grp][0]

        def rows_of(rows, grp):
            n0, nb = units[grp[0]]
            return rows[n0 * B:(n0 + nb * len(grp)) * B, :].rearrange("(j q e) f -> q j (e f)", j=len(grp), e=nb)

        def load_x(s):
            grp = group_of(x_groups, s)
            if s != grp[0]:
                return
            n0, nb = units[s]
            both = raw.tile([P, 2, 2, K], BF16, name="xraw", tag="xraw")
            nc.sync.dma_start(
                out=both[:, 0:len(grp), 0:nb, :].rearrange("q j e k -> q j (e k)"), in_=rows_of(x_rows, grp)
            )
            for j in range(len(grp)):
                xraw[grp[j]] = both[:, j]

        def load_w(s):
            n0, nb = units[s]
            wraw[s] = raw.tile([P, 4, K], BF16, name="wraw", tag="wraw")
            nc.sync.dma_start(out=wraw[s][:, 0:2 * nb, :], in_=w_hbm[:, 2 * n0:2 * (n0 + nb), :])

        def load_p(s):
            grp = group_of(p_groups, s)
            if s != grp[0]:
                return
            n0, nb = units[s]
            both = raw.tile([P, 2, 2, T, C], BF16, name="praw", tag="praw")
            nc.sync.dma_start(
                out=both[:, 0:len(grp), 0:nb].rearrange("q j e t c -> q j (e t c)"), in_=rows_of(p_rows, grp)
            )
            for j in range(len(grp)):
                praw[grp[j]] = both[:, j]

        def transposes(s):
            n0, nb = units[s]
            if nb == 1:
                words = xraw[s][:, 0, :].bitcast(F32)
                bank = ps_t.tile([P, 2, 2, B], F32, name="xt", tag="xt")
                for g in range(2):
                    for u in range(2):
                        nc.tensor.transpose(bank[:, g, u, :], words[:, 256 * g + u:256 * (g + 1):2], ident[:])
                xt[(s, 0)] = bank
            else:
                for g in range(2):
                    bank = ps_t.tile([P, 2, 2, B], F32, name="xt", tag="xt")
                    for u in range(2):
                        for e in range(2):
                            words = xraw[s][:, e, :].bitcast(F32)
                            nc.tensor.transpose(bank[:, u, e, :], words[:, 256 * g + u:256 * (g + 1):2], ident[:])
                    xt[(s, g)] = bank

        def evac(s):
            n0, nb = units[s]
            xg[s] = mid.tile([P, 2 * K], BF16, name="xg", tag="xg", align_bytes=64)
            if nb == 1:
                nc.scalar.copy(
                    out=xg[s][:, 0:K].bitcast(F32).rearrange("p (g q u) -> p g q u", g=2, u=2),
                    in_=xt[(s, 0)][:].rearrange("p g u q -> p g q u"),
                )
            else:
                for g in range(2):
                    nc.scalar.copy(
                        out=xg[s][:, g * K:(g + 1) * K].bitcast(F32).rearrange("p (e q u) -> p e q u", e=2, u=2),
                        in_=xt[(s, g)][:].rearrange("p u e q -> p e q u"),
                    )

        def w_src(s, a0, a1, c0, c1):
            return wraw[s][:, a0:a1, :].rearrange("q a (j c i) -> q a c j i", j=4, i=4)[:, :, c0 // 4:c1 // 4, :, :]

        def w_dst(s, a0, a1, c0, c1):
            return wg[s][:, a0:a1].rearrange("q a (c i) j -> q a c j i", i=4)[:, :, c0 // 4:c1 // 4, :, :]

        def inter_v(s):
            n0, nb = units[s]
            wg[s] = wgp.tile([P, 4, C, 4], BF16, name="wg", tag="wg", align_bytes=64)
            nc.vector.tensor_copy(out=w_dst(s, 0, 2 * nb, 0, cv_of(s)), in_=w_src(s, 0, 2 * nb, 0, cv_of(s)))

        def inter_s(s, i):
            n0, nb = units[s]
            if i < nb:
                nc.scalar.copy(out=w_dst(s, 2 * i, 2 * i + 2, cv_of(s), C), in_=w_src(s, 2 * i, 2 * i + 2, cv_of(s), C))

        def quant_x(s):
            n0, nb = units[s]
            if nb == 1:
                xc[s] = mid.tile([P, 2 * B], U32, name="xc", tag="xc", align_bytes=64)
                xs[s] = mid.tile([P, 2 * B], U8, name="xs", tag="xs", align_bytes=64)
                nc.vector.quantize_mx(out=xc[s][:].bitcast(FP8X4), scales=xs[s][:], in_=xg[s][:, 0:K])
                return
            xc[s] = xc_keep[s % 2]
            xs[s] = xs_keep[s % 2]
            runs = [(0, 1, 0)] + [(2 * r - 1, 2, 3 * r - 1) for r in (1, 2, 3)] + [(7, 1, 11)]
            for src, n, dst in runs:
                nc.vector.quantize_mx(
                    out=xc[s][:, dst * H:(dst + n) * H].bitcast(FP8X4),
                    scales=xs[s][:, dst * H:(dst + n) * H],
                    in_=xg[s][:, src * 4 * H:(src + n) * 4 * H],
                )

        def quant_w(s):
            n0, nb = units[s]
            wc[s] = mid.tile([P, 4 * C], U32, name="wc", tag="wc", align_bytes=64)
            ws[s] = mid.tile([P, 4 * C], U8, name="ws", tag="ws", align_bytes=64)
            for i in range(nb):
                cols = slice(2 * i * C, (2 * i + 2) * C)
                nc.vector.quantize_mx(
                    out=wc[s][:, cols].bitcast(FP8X4),
                    scales=ws[s][:, cols],
                    in_=wg[s][:, 2 * i:2 * i + 2].rearrange("q a c j -> q (a c j)"),
                )

        def matmuls(s):
            n0, nb = units[s]
            yb[s] = ps_y.tile([P, 2 * C], F32, name="yb", tag="yb")
            if nb == 1:
                for g in range(2):
                    nc.tensor.matmul_mx(
                        out=yb[s][:, 0:C],
                        lhsT=xc[s][:, g * B:(g + 1) * B].bitcast(FP8X4),
                        lhsT_scale=xs[s][:, g * B:(g + 1) * B],
                        rhs=wc[s][:, g * C:(g + 1) * C].bitcast(FP8X4),
                        rhs_scale=ws[s][:, g * C:(g + 1) * C],
                        start=(g == 0),
                        stop=(g == 1),
                    )
                return
            for e in range(2):
                for i in range(2):
                    for g in range(2):
                        a = 2 * i + g
                        x0 = (3 * (2 * g + e) + i) * H
                        nc.tensor.matmul_mx(
                            out=yb[s][:, e * C:(e + 1) * C],
                            lhsT=xc[s][:, x0:x0 + B].bitcast(FP8X4),
                            lhsT_scale=xs[s][:, x0:x0 + B],
                            rhs=wc[s][:, a * C:(a + 1) * C].bitcast(FP8X4),
                            rhs_scale=ws[s][:, a * C:(a + 1) * C],
                            start=(i == 0 and g == 0),
                            stop=(i == 1 and g == 1),
                        )

        def slope(s):
            n0, nb = units[s]
            w = nb * C
            tt[s] = epi.tile([P, 2 * C], F32, name="tt", tag="tt")
            nc.scalar.activation(out=tt[s][:, 0:w], in_=yb[s][:, 0:w], func=ACT.Copy, scale=SLOPE)

        def leaky(s):
            n0, nb = units[s]
            w = nb * C
            uu[s] = epi.tile([P, 2 * C], F32, name="uu", tag="uu")
            nc.vector.tensor_tensor(out=uu[s][:, 0:w], in0=yb[s][:, 0:w], in1=tt[s][:, 0:w], op=ALU.max)

        def pmax1(s):
            n0, nb = units[s]
            m1[s] = epi.tile([P, 2, 2, C], BF16, name="m1", tag="m1")
            nc.vector.tensor_tensor(
                out=m1[s][:, 0:nb], in0=praw[s][:, 0:nb, 0:2, :], in1=praw[s][:, 0:nb, 2:4, :], op=ALU.max
            )

        def pmax2(s):
            n0, nb = units[s]
            m2[s] = epi.tile([P, 2, C], BF16, name="m2", tag="m2")
            nc.vector.tensor_tensor(
                out=m2[s][:, 0:nb], in0=m1[s][:, 0:nb, 0, :], in1=m1[s][:, 0:nb, 1, :], op=ALU.max
            )

        def add_p(s):
            n0, nb = units[s]
            w = nb * C
            grp = group_of(po_groups, s)
            if s == grp[0]:
                oo_both[s] = late.tile([P, 2, 2 * C], F32, name="oo", tag="oo")
                for j in range(len(grp)):
                    oo[grp[j]] = oo_both[s][:, j]
            nc.vector.tensor_tensor(
                out=oo[s][:, 0:w], in0=uu[s][:, 0:w], in1=m2[s][:, 0:nb].rearrange("b n c -> b (n c)"), op=ALU.add
            )

        def cast(s):
            n0, nb = units[s]
            w = nb * C
            grp = group_of(po_groups, s)
            if s == grp[0]:
                f8_both[s] = late.tile([P, 2, 2 * C], FP8, name="f8", tag="f8")
                for j in range(len(grp)):
                    f8[grp[j]] = f8_both[s][:, j]
            nc.scalar.activation(out=f8[s][:, 0:w], in_=oo[s][:, 0:w], func=ACT.Copy, scale=Y_SCALE, saturate=False)

        def store(s):
            grp = group_of(po_groups, s)
            if s != grp[-1]:
                return
            n0, nb = units[s]
            w = nb * C
            nc.sync.dma_start(out=rows_of(o0_rows, grp), in_=oo_both[grp[0]][:, 0:len(grp), 0:w])
            nc.sync.dma_start(out=rows_of(o1_rows, grp), in_=f8_both[grp[0]][:, 0:len(grp), 0:w].bitcast(U8))

        def body():
            for s in range(-2, U + SLAG + 1):
                if ok(s + 1):
                    load_x(s + 1)
                    load_w(s + 1)
                if ok(s + 1 - PLAG):
                    load_p(s + 1 - PLAG)
                if ok(s - SLAG):
                    store(s - SLAG)
                if ok(s - LLAG):
                    slope(s - LLAG)
                if ok(s):
                    inter_v(s)
                    inter_s(s, 0)
                if ok(s):
                    inter_s(s, 1)
                if ok(s - PLAG):
                    pmax1(s - PLAG)
                if ok(s - LLAG):
                    leaky(s - LLAG)
                if ok(s - PLAG):
                    pmax2(s - PLAG)
                if ok(s + 1 - QLAG):
                    transposes(s + 1 - QLAG)
                    evac(s + 1 - QLAG)
                if ok(s - QLAG):
                    quant_x(s - QLAG)
                if ok(s - PLAG):
                    add_p(s - PLAG)
                    cast(s - PLAG)
                if ok(s - QLAG):
                    quant_w(s - QLAG)
                    matmuls(s - QLAG)

        if MANUAL:
            with tc.manual_schedule():
                body()
        else:
            body()
